import numpy as np
import ml_dtypes


def mxq(x, axis, fmt="e4m3"):
    dtype, down = {"e4m3": (ml_dtypes.float8_e4m3fn, 7), "e5m2": (ml_dtypes.float8_e5m2, 14)}[fmt]
    v = np.moveaxis(np.asarray(x, np.float32).astype(ml_dtypes.bfloat16).astype(np.float64), axis, -1)
    blocks = v.reshape(v.shape[:-1] + (-1, 32))
    amax = np.abs(blocks).max(-1, keepdims=True)
    byte = np.maximum(np.where(amax > 0, np.frexp(amax)[1] - 1 + 127, 0) - down, 1)
    scale = np.exp2(byte - 127.0)
    codes = (blocks / scale).astype(np.float32).astype(dtype).astype(np.float64)
    return np.moveaxis((codes * scale).reshape(v.shape), -1, axis)


WIDE = False


def mx_kscale(k):
    if not WIDE:
        return np.ones(k)
    levels = np.array([10, -10, 5, -5, 0])
    a = np.random.permutation(np.resize(levels, k // 512 * 4)).reshape(k // 512, 4)
    idx = np.arange(k)
    return np.exp2(a[idx // 512, idx % 128 // 32])


BF16 = ml_dtypes.bfloat16


def bf(x):
    return np.asarray(x, np.float32).astype(BF16)


def f64(x):
    return np.asarray(x).astype(np.float64)


B, A, E, P, R = 256, 8, 512, 512, 512


def setup_inputs():
    s_src, s_edge = mx_kscale(E), mx_kscale(E)
    t = mx_kscale(P)
    s_cat = np.concatenate([s_src, s_edge])
    return {
        "image_features": bf(np.random.standard_normal((B, E)) * s_src),
        "edge_attributes": bf(np.random.standard_normal((B, A, E)) * s_edge),
        "linear_w": bf(np.random.standard_normal((P, 2 * E)) / np.sqrt(2 * E) / s_cat * t[:, None]),
        "linear_b": bf(np.random.standard_normal(P) * 0.3 * t),
        "fwd_proj": bf(np.random.standard_normal((A, P, R)) / np.sqrt(P) / t[:, None]),
    }


def reference(image_features, edge_attributes, linear_w, linear_b, fwd_proj):
    w = f64(linear_w)
    node = mxq(f64(image_features), 1, "e4m3") @ mxq(w[:, :E].T, 0, "e4m3")
    edge = (mxq(f64(edge_attributes).reshape(B * A, E), 1, "e4m3") @ mxq(w[:, E:].T, 0, "e4m3")).reshape(B, A, P)
    agg = node[:, None, :] + edge + f64(linear_b)
    rep = mxq(agg.transpose(1, 0, 2), 2, "e4m3") @ mxq(f64(fwd_proj), 1, "e4m3")
    return rep.transpose(1, 0, 2)

@@ -1,0 +1,254 @@
+from contextlib import ExitStack
+
+import concourse.mybir as mybir
+from concourse.masks import make_identity
+
+F32 = mybir.dt.float32
+BF16 = mybir.dt.bfloat16
+U32 = mybir.dt.uint32
+U8 = mybir.dt.uint8
+FP8X4 = mybir.dt.float8_e4m3fn_x4
+ADD = mybir.AluOpType.add
+
+NB, NA, NE, NP, NR = 256, 8, 512, 512, 512
+PT = 128
+FLOPS = 2 * (NB * NE * NP + NB * NA * NE * NP + NB * NA * NP * NR)
+
+V_COLS = 256
+
+
+def tile_attributegnn_pa_kernel(
+    tc, image_features, edge_attributes, linear_w, linear_b, fwd_proj, out
+):
+    nc = tc.nc
+    with ExitStack() as ctx:
+        keep = ctx.enter_context(tc.tile_pool(name="keep", bufs=1))
+        rot = ctx.enter_context(tc.tile_pool(name="rot", bufs=3))
+        outp = ctx.enter_context(tc.tile_pool(name="outp", bufs=4))
+        ps_tr = ctx.enter_context(tc.psum_pool(name="ps_tr", bufs=2))
+        ps_s1 = ctx.enter_context(tc.psum_pool(name="ps_s1", bufs=3))
+        ps_s2 = ctx.enter_context(tc.psum_pool(name="ps_s2", bufs=3))
+        ctx.enter_context(tc.manual_schedule())
+
+        w_v = linear_w.rearrange("(p t) e -> p t e", t=4)
+        img_v = image_features.rearrange("(p bt) e -> p (bt e)", bt=2)
+        edge_v = edge_attributes.rearrange("(p bt) a e -> p bt (a e)", bt=2)
+        fwd_v = fwd_proj.rearrange("a (p t) r -> a p (t r)", t=4)
+        b_v = linear_b.rearrange("(p t) -> p t", t=4)
+        out_v = out.rearrange("(p bt) a r -> p bt a r", bt=2)
+
+        w_sb = keep.tile([PT, 4 * 1024], BF16, name="w_sb")
+        img_sb = keep.tile([PT, 1024], BF16, name="img_sb")
+        bias_bf = keep.tile([PT, 4], BF16, name="bias_bf")
+        bias_f = keep.tile([PT, 4], F32, name="bias_f")
+        e_sb = [keep.tile([PT, 2048], BF16, name="e_sb%d" % q) for q in range(4)]
+        f_sb = [keep.tile([PT, 2048], BF16, name="f_sb%d" % a) for a in range(NA)]
+        ident = keep.tile([PT, PT], F32, name="ident")
+
+        w_g = keep.tile([PT, 4096], BF16, name="w_g", align_bytes=64)
+        w_c = keep.tile([PT, 1024], U32, name="w_c", align_bytes=64)
+        w_s = keep.tile([PT, 1024], U8, name="w_s", align_bytes=64)
+        img_g = keep.tile([PT, 1024], BF16, name="img_g", align_bytes=64)
+        img_c = keep.tile([PT, 256], U32, name="img_c", align_bytes=64)
+        img_s = keep.tile([PT, 256], U8, name="img_s", align_bytes=64)
+        e_c = keep.tile([PT, NA * 256], U32, name="e_c", align_bytes=64)
+        e_s = keep.tile([PT, NA * 256], U8, name="e_s", align_bytes=64)
+        a_c = keep.tile([PT, NA * 256], U32, name="a_c", align_bytes=64)
+        a_s = keep.tile([PT, NA * 256], U8, name="a_s", align_bytes=64)
+        f_c = keep.tile([PT, NA * 512], U32, name="f_c", align_bytes=64)
+        f_s = keep.tile([PT, NA * 512], U8, name="f_s", align_bytes=64)
+        nodeb = keep.tile([PT, 1024], F32, name="nodeb")
+
+        for t in range(4):
+            nc.sync.dma_start(out=w_sb[:, t * 1024:(t + 1) * 1024], in_=w_v[:, t, :])
+        nc.sync.dma_start(out=img_sb[:], in_=img_v)
+        nc.sync.dma_start(out=bias_bf[:], in_=b_v)
+
+        def load_edge(q):
+            nc.sync.dma_start(
+                out=e_sb[q][:].rearrange("p (bt x) -> p bt x", bt=2),
+                in_=edge_v[:, :, q * 1024:(q + 1) * 1024],
+            )
+
+        def load_fwd(a):
+            nc.sync.dma_start(out=f_sb[a][:], in_=fwd_v[a])
+
+        for q in range(4):
+            load_edge(q)
+            load_fwd(2 * q)
+            load_fwd(2 * q + 1)
+
+        make_identity(nc, ident[:])
+        nc.vector.tensor_copy(out=bias_f[:], in_=bias_bf[:])
+
+        def transpose_words(dst, src32, cols):
+            nc.tensor.transpose(dst, src32[:, cols:cols + PT], ident[:])
+
+        def quantise(codes, scales, grouped):
+            nc.vector.quantize_mx(out=codes.bitcast(FP8X4), scales=scales, in_=grouped)
+
+        def mx(acc, lc, ls, rc, rs):
+            nc.tensor.matmul_mx(
+                out=acc, lhsT=lc.bitcast(FP8X4), lhsT_scale=ls,
+                rhs=rc.bitcast(FP8X4), rhs_scale=rs, start=True, stop=True,
+            )
+
+        w32 = w_sb[:].bitcast(F32)
+        wg32 = w_g[:].bitcast(F32)
+        live = {}
+
+        def t_w(t):
+            tr = ps_tr.tile([PT, 512], F32, name="tr", tag="tr")
+            for hu in range(4):
+                transpose_words(tr[:, hu * PT:(hu + 1) * PT], w32, t * 512 + hu * PT)
+            live["tw", t] = tr
+
+        def e_w(t):
+            nc.scalar.copy(
+                out=wg32[:, t * 512:(t + 1) * 512].rearrange("p (h m u) -> p h m u", h=2, u=2),
+                in_=live["tw", t][:].rearrange("p (h u m) -> p h m u", h=2, u=2),
+            )
+
+        def q_w(t):
+            quantise(w_c[:, t * 256:(t + 1) * 256], w_s[:, t * 256:(t + 1) * 256],
+                     w_g[:, t * 1024:(t + 1) * 1024])
+
+        def t_rows(key, src32, stride_bt, base):
+            tr = ps_tr.tile([PT, 512], F32, name="tr", tag="tr")
+            for u in range(2):
+                for bt in range(2):
+                    transpose_words(tr[:, u * 256 + bt * PT: u * 256 + (bt + 1) * PT],
+                                    src32, bt * stride_bt + base + u * PT)
+            live[key] = tr
+
+        def e_rows(key, grouped):
+            nc.scalar.copy(
+                out=grouped[:].bitcast(F32).rearrange("p (c u) -> p c u", u=2),
+                in_=live[key][:].rearrange("p (u c) -> p c u", u=2),
+            )
+
+        def t_e(a):
+            t_rows(("te", a), e_sb[a // 2][:].bitcast(F32), 512, (a % 2) * 256)
+
+        def e_e(a):
+            eg = rot.tile([PT, 1024], BF16, name="eg", tag="eg", align_bytes=64)
+            e_rows(("te", a), eg)
+            live["eg", a] = eg
+
+        def q_e(a):
+            quantise(e_c[:, a * 256:(a + 1) * 256], e_s[:, a * 256:(a + 1) * 256],
+                     live["eg", a][:])
+
+        def stage1(key, h, rc, rs):
+            for bt in range(2):
+                acc = ps_s1.tile([PT, 512], F32, name="s1", tag="s1")
+                for t in range(4):
+                    o = t * 256 + h * PT
+                    mx(acc[:, t * PT:(t + 1) * PT], w_c[:, o:o + PT], w_s[:, o:o + PT],
+                       rc[:, bt * PT:(bt + 1) * PT], rs[:, bt * PT:(bt + 1) * PT])
+                live[key, bt] = acc
+
+        def n_ev(bt):
+            nc.vector.tensor_tensor(
+                out=nodeb[:, bt * 512:(bt + 1) * 512].rearrange("p (c t) -> p c t", t=4),
+                in0=live["n", bt][:].rearrange("p (t c) -> p c t", t=4),
+                in1=bias_f[:].unsqueeze(1).to_broadcast([PT, PT, 4]),
+                op=ADD,
+            )
+
+        def s1(a):
+            stage1(("s1", a), 1, e_c[:, a * 256:(a + 1) * 256], e_s[:, a * 256:(a + 1) * 256])
+
+        def a_v(a):
+            ag = rot.tile([PT, 1024], BF16, name="ag", tag="ag", align_bytes=64)
+            for bt in range(2):
+                nc.vector.tensor_tensor(
+                    out=ag[:, bt * 512:(bt + 1) * 512].rearrange("p (c t) -> p c t", t=4),
+                    in0=live[("s1", a), bt][:].rearrange("p (t c) -> p c t", t=4),
+                    in1=nodeb[:, bt * 512:(bt + 1) * 512].rearrange("p (c t) -> p c t", t=4),
+                    op=ADD,
+                )
+            live["ag", a] = ag
+
+        def q_a(a):
+            quantise(a_c[:, a * 256:(a + 1) * 256], a_s[:, a * 256:(a + 1) * 256],
+                     live["ag", a][:])
+
+        def rg_views(a, r0, r1):
+            fg = live["fg", a]
+            dst = fg[:, r0 * 4:r1 * 4].rearrange("p (c i t) -> p c t i", i=4, t=4)
+            src = f_sb[a][:].rearrange("p (t r) -> p t r", t=4)[:, :, r0:r1].rearrange(
+                "p t (c i) -> p c t i", i=4)
+            return dst, src
+
+        def rg_s(a):
+            live["fg", a] = rot.tile([PT, 2048], BF16, name="fg", tag="fg", align_bytes=64)
+            dst, src = rg_views(a, V_COLS, NR)
+            nc.scalar.copy(out=dst, in_=src)
+
+        def rg_v(a):
+            dst, src = rg_views(a, 0, V_COLS)
+            nc.vector.tensor_copy(out=dst, in_=src)
+
+        def q_f(a):
+            quantise(f_c[:, a * 512:(a + 1) * 512], f_s[:, a * 512:(a + 1) * 512],
+                     live["fg", a][:])
+
+        def s2(a):
+            for bt in range(2):
+                acc = ps_s2.tile([PT, 512], F32, name="s2", tag="s2")
+                o = a * 256 + bt * PT
+                mx(acc[:], a_c[:, o:o + PT], a_s[:, o:o + PT],
+                   f_c[:, a * 512:(a + 1) * 512], f_s[:, a * 512:(a + 1) * 512])
+                live["s2", a, bt] = acc
+
+        def o_s(a):
+            o_sb = outp.tile([PT, 1024], F32, name="o_sb", tag="o_sb")
+            for bt in range(2):
+                nc.scalar.copy(out=o_sb[:, bt * 512:(bt + 1) * 512], in_=live["s2", a, bt][:])
+            nc.sync.dma_start(out=out_v[:, :, a, :],
+                              in_=o_sb[:].rearrange("p (bt r) -> p bt r", bt=2))
+
+        for t in range(4):
+            t_w(t)
+            e_w(t)
+            q_w(t)
+        t_rows("ti", img_sb[:].bitcast(F32), 256, 0)
+        e_rows("ti", img_g)
+        quantise(img_c[:], img_s[:], img_g[:])
+        t_e(0)
+        e_e(0)
+        stage1("n", 0, img_c, img_s)
+
+        for i in range(-1, NA):
+            if i + 2 < NA:
+                t_e(i + 2)
+            if i + 1 < NA:
+                rg_s(i + 1)
+            if i >= 0:
+                a_v(i)
+            if i >= 1:
+                o_s(i - 1)
+            if i + 1 < NA:
+                q_e(i + 1)
+            if i == -1:
+                n_ev(0)
+                n_ev(1)
+            if i + 1 < NA:
+                s1(i + 1)
+            if i + 1 < NA:
+                rg_v(i + 1)
+            if i >= 0:
+                q_a(i)
+                s2(i)
+            if i + 2 < NA:
+                e_e(i + 2)
+            if i + 1 < NA:
+                q_f(i + 1)
+
+        last = NA - 1
+        o_last = outp.tile([PT, 1024], F32, name="o_sb", tag="o_sb")
+        nc.scalar.copy(out=o_last[:, 0:512], in_=live["s2", last, 0][:])
+        nc.vector.tensor_copy(out=o_last[:, 512:1024], in_=live["s2", last, 1][:])
+        for bt in range(2):
+            nc.sync.dma_start(out=out_v[:, bt, last, :], in_=o_last[:, bt * 512:(bt + 1) * 512])

@@ -14,7 +14,7 @@ NB, NA, NE, NP, NR = 256, 8, 512, 512, 512
 PT = 128
 FLOPS = 2 * (NB * NE * NP + NB * NA * NE * NP + NB * NA * NP * NR)
 
-V_COLS = 256
+V_COLS = 224
 
 
 def tile_attributegnn_pa_kernel(
@@ -23,11 +23,9 @@ def tile_attributegnn_pa_kernel(
     nc = tc.nc
     with ExitStack() as ctx:
         keep = ctx.enter_context(tc.tile_pool(name="keep", bufs=1))
-        rot = ctx.enter_context(tc.tile_pool(name="rot", bufs=3))
+        rot = ctx.enter_context(tc.tile_pool(name="rot", bufs=4))
         outp = ctx.enter_context(tc.tile_pool(name="outp", bufs=4))
-        ps_tr = ctx.enter_context(tc.psum_pool(name="ps_tr", bufs=2))
-        ps_s1 = ctx.enter_context(tc.psum_pool(name="ps_s1", bufs=3))
-        ps_s2 = ctx.enter_context(tc.psum_pool(name="ps_s2", bufs=3))
+        psum = ctx.enter_context(tc.psum_pool(name="psum", bufs=8))
         ctx.enter_context(tc.manual_schedule())
 
         w_v = linear_w.rearrange("(p t) e -> p t e", t=4)
@@ -79,7 +77,6 @@ def tile_attributegnn_pa_kernel(
             load_fwd(2 * q + 1)
 
         make_identity(nc, ident[:])
-        nc.vector.tensor_copy(out=bias_f[:], in_=bias_bf[:])
 
         def transpose_words(dst, src32, cols):
             nc.tensor.transpose(dst, src32[:, cols:cols + PT], ident[:])
@@ -98,13 +95,20 @@ def tile_attributegnn_pa_kernel(
         live = {}
 
         def t_w(t):
-            tr = ps_tr.tile([PT, 512], F32, name="tr", tag="tr")
+            tr = psum.tile([PT, 512], F32, name="tr", tag="bank")
             for hu in range(4):
                 transpose_words(tr[:, hu * PT:(hu + 1) * PT], w32, t * 512 + hu * PT)
             live["tw", t] = tr
 
-        def e_w(t):
-            nc.scalar.copy(
+        def copy_on(eng, out, in_):
+            if eng == "V":
+                nc.vector.tensor_copy(out=out, in_=in_)
+            else:
+                nc.scalar.copy(out=out, in_=in_)
+
+        def e_w(t, eng):
+            copy_on(
+                eng,
                 out=wg32[:, t * 512:(t + 1) * 512].rearrange("p (h m u) -> p h m u", h=2, u=2),
                 in_=live["tw", t][:].rearrange("p (h u m) -> p h m u", h=2, u=2),
             )
@@ -114,7 +118,7 @@ def tile_attributegnn_pa_kernel(
                      w_g[:, t * 1024:(t + 1) * 1024])
 
         def t_rows(key, src32, stride_bt, base):
-            tr = ps_tr.tile([PT, 512], F32, name="tr", tag="tr")
+            tr = psum.tile([PT, 512], F32, name="tr", tag="bank")
             for u in range(2):
                 for bt in range(2):
                     transpose_words(tr[:, u * 256 + bt * PT: u * 256 + (bt + 1) * PT],
@@ -141,7 +145,7 @@ def tile_attributegnn_pa_kernel(
 
         def stage1(key, h, rc, rs):
             for bt in range(2):
-                acc = ps_s1.tile([PT, 512], F32, name="s1", tag="s1")
+                acc = psum.tile([PT, 512], F32, name="s1", tag="bank")
                 for t in range(4):
                     o = t * 256 + h * PT
                     mx(acc[:, t * PT:(t + 1) * PT], w_c[:, o:o + PT], w_s[:, o:o + PT],
@@ -175,6 +179,8 @@ def tile_attributegnn_pa_kernel(
                      live["ag", a][:])
 
         def rg_views(a, r0, r1):
+            if ("fg", a) not in live:
+                live["fg", a] = rot.tile([PT, 2048], BF16, name="fg", tag="fg", align_bytes=64)
             fg = live["fg", a]
             dst = fg[:, r0 * 4:r1 * 4].rearrange("p (c i t) -> p c t i", i=4, t=4)
             src = f_sb[a][:].rearrange("p (t r) -> p t r", t=4)[:, :, r0:r1].rearrange(
@@ -182,7 +188,6 @@ def tile_attributegnn_pa_kernel(
             return dst, src
 
         def rg_s(a):
-            live["fg", a] = rot.tile([PT, 2048], BF16, name="fg", tag="fg", align_bytes=64)
             dst, src = rg_views(a, V_COLS, NR)
             nc.scalar.copy(out=dst, in_=src)
 
@@ -196,59 +201,72 @@ def tile_attributegnn_pa_kernel(
 
         def s2(a):
             for bt in range(2):
-                acc = ps_s2.tile([PT, 512], F32, name="s2", tag="s2")
+                acc = psum.tile([PT, 512], F32, name="s2", tag="bank")
                 o = a * 256 + bt * PT
                 mx(acc[:], a_c[:, o:o + PT], a_s[:, o:o + PT],
                    f_c[:, a * 512:(a + 1) * 512], f_s[:, a * 512:(a + 1) * 512])
                 live["s2", a, bt] = acc
 
-        def o_s(a):
+        def o_ev(a, engines, split_store):
             o_sb = outp.tile([PT, 1024], F32, name="o_sb", tag="o_sb")
             for bt in range(2):
-                nc.scalar.copy(out=o_sb[:, bt * 512:(bt + 1) * 512], in_=live["s2", a, bt][:])
-            nc.sync.dma_start(out=out_v[:, :, a, :],
-                              in_=o_sb[:].rearrange("p (bt r) -> p bt r", bt=2))
+                copy_on(engines[bt], out=o_sb[:, bt * 512:(bt + 1) * 512], in_=live["s2", a, bt][:])
+            if split_store:
+                for bt in range(2):
+                    nc.sync.dma_start(out=out_v[:, bt, a, :], in_=o_sb[:, bt * 512:(bt + 1) * 512])
+            else:
+                nc.sync.dma_start(out=out_v[:, :, a, :],
+                                  in_=o_sb[:].rearrange("p (bt r) -> p bt r", bt=2))
 
-        for t in range(4):
-            t_w(t)
-            e_w(t)
-            q_w(t)
+        t_w(0)
+        e_w(0, "S")
+        t_w(1)
+        e_w(1, "V")
+        q_w(0)
+        t_w(2)
+        e_w(2, "S")
+        q_w(1)
+        t_w(3)
+        e_w(3, "V")
+        q_w(2)
         t_rows("ti", img_sb[:].bitcast(F32), 256, 0)
         e_rows("ti", img_g)
-        quantise(img_c[:], img_s[:], img_g[:])
+        q_w(3)
+        nc.vector.tensor_copy(out=bias_f[:], in_=bias_bf[:])
         t_e(0)
         e_e(0)
+        quantise(img_c[:], img_s[:], img_g[:])
         stage1("n", 0, img_c, img_s)
+        t_e(1)
+        rg_s(0)
+        rg_v(0)
+        q_e(0)
+        s1(0)
+        e_e(1)
+        rg_v(1)
+        n_ev(0)
+        n_ev(1)
+        rg_s(1)
+        q_f(0)
 
-        for i in range(-1, NA):
+        for i in range(NA):
             if i + 2 < NA:
                 t_e(i + 2)
-            if i + 1 < NA:
-                rg_s(i + 1)
-            if i >= 0:
-                a_v(i)
-            if i >= 1:
-                o_s(i - 1)
+            a_v(i)
+            if i >= 2:
+                o_ev(i - 2, "SS", False)
             if i + 1 < NA:
                 q_e(i + 1)
-            if i == -1:
-                n_ev(0)
-                n_ev(1)
-            if i + 1 < NA:
                 s1(i + 1)
-            if i + 1 < NA:
-                rg_v(i + 1)
-            if i >= 0:
-                q_a(i)
-                s2(i)
+            if i + 2 < NA:
+                rg_s(i + 2)
+                rg_v(i + 2)
+            q_a(i)
+            s2(i)
             if i + 2 < NA:
                 e_e(i + 2)
             if i + 1 < NA:
                 q_f(i + 1)
 
-        last = NA - 1
-        o_last = outp.tile([PT, 1024], F32, name="o_sb", tag="o_sb")
-        nc.scalar.copy(out=o_last[:, 0:512], in_=live["s2", last, 0][:])
-        nc.vector.tensor_copy(out=o_last[:, 512:1024], in_=live["s2", last, 1][:])
-        for bt in range(2):
-            nc.sync.dma_start(out=out_v[:, bt, last, :], in_=o_last[:, bt * 512:(bt + 1) * 512])
+        o_ev(NA - 2, "SV", False)
+        o_ev(NA - 1, "SV", True)

@@ -14,7 +14,7 @@ NB, NA, NE, NP, NR = 256, 8, 512, 512, 512
 PT = 128
 FLOPS = 2 * (NB * NE * NP + NB * NA * NE * NP + NB * NA * NP * NR)
 
-V_COLS = 224
+V_COLS = 192
 
 
 def tile_attributegnn_pa_kernel(

@@ -178,6 +178,10 @@ def tile_attributegnn_pa_kernel(
             quantise(a_c[:, a * 256:(a + 1) * 256], a_s[:, a * 256:(a + 1) * 256],
                      live["ag", a][:])
 
+        def q_a_half(a, bt):
+            o = a * 256 + bt * PT
+            quantise(a_c[:, o:o + PT], a_s[:, o:o + PT], live["ag", a][:, bt * 512:(bt + 1) * 512])
+
         def rg_views(a, r0, r1):
             if ("fg", a) not in live:
                 live["fg", a] = rot.tile([PT, 2048], BF16, name="fg", tag="fg", align_bytes=64)
@@ -199,13 +203,16 @@ def tile_attributegnn_pa_kernel(
             quantise(f_c[:, a * 512:(a + 1) * 512], f_s[:, a * 512:(a + 1) * 512],
                      live["fg", a][:])
 
+        def s2_cols(a, bt, c0, c1):
+            acc = psum.tile([PT, 512], F32, name="s2", tag="bank")
+            o = a * 256 + bt * PT
+            mx(acc[:, 0:c1 - c0], a_c[:, o:o + PT], a_s[:, o:o + PT],
+               f_c[:, a * 512 + c0:a * 512 + c1], f_s[:, a * 512 + c0:a * 512 + c1])
+            return acc
+
         def s2(a):
             for bt in range(2):
-                acc = psum.tile([PT, 512], F32, name="s2", tag="bank")
-                o = a * 256 + bt * PT
-                mx(acc[:], a_c[:, o:o + PT], a_s[:, o:o + PT],
-                   f_c[:, a * 512:(a + 1) * 512], f_s[:, a * 512:(a + 1) * 512])
-                live["s2", a, bt] = acc
+                live["s2", a, bt] = s2_cols(a, bt, 0, NR)
 
         def o_ev(a, engines, split_store):
             o_sb = outp.tile([PT, 1024], F32, name="o_sb", tag="o_sb")
@@ -261,12 +268,30 @@ def tile_attributegnn_pa_kernel(
             if i + 2 < NA:
                 rg_s(i + 2)
                 rg_v(i + 2)
-            q_a(i)
-            s2(i)
+            if i + 1 < NA:
+                q_a(i)
+                s2(i)
             if i + 2 < NA:
                 e_e(i + 2)
             if i + 1 < NA:
                 q_f(i + 1)
 
-        o_ev(NA - 2, "SV", False)
-        o_ev(NA - 1, "SV", True)
+        last = NA - 1
+        q_a_half(last, 0)
+        acc_a = s2_cols(last, 0, 0, NR)
+        q_a_half(last, 1)
+        acc_b = s2_cols(last, 1, 0, 256)
+        acc_c = s2_cols(last, 1, 256, NR)
+
+        o_6 = outp.tile([PT, 1024], F32, name="o_sb", tag="o_sb")
+        o_7 = outp.tile([PT, 1024], F32, name="o_sb", tag="o_sb")
+        nc.scalar.copy(out=o_6[:, 0:512], in_=live["s2", last - 1, 0][:])
+        nc.sync.dma_start(out=out_v[:, 0, last - 1, :], in_=o_6[:, 0:512])
+        nc.vector.tensor_copy(out=o_6[:, 512:1024], in_=live["s2", last - 1, 1][:])
+        nc.sync.dma_start(out=out_v[:, 1, last - 1, :], in_=o_6[:, 512:1024])
+        nc.scalar.copy(out=o_7[:, 0:512], in_=acc_a[:])
+        nc.sync.dma_start(out=out_v[:, 0, last, :], in_=o_7[:, 0:512])
+        nc.vector.tensor_copy(out=o_7[:, 512:768], in_=acc_b[:, 0:256])
+        nc.sync.dma_start(out=out_v[:, 1, last, 0:256], in_=o_7[:, 512:768])
+        nc.scalar.copy(out=o_7[:, 768:1024], in_=acc_c[:, 0:256])
+        nc.sync.dma_start(out=out_v[:, 1, last, 256:512], in_=o_7[:, 768:1024])

@@ -14,7 +14,7 @@ NB, NA, NE, NP, NR = 256, 8, 512, 512, 512
 PT = 128
 FLOPS = 2 * (NB * NE * NP + NB * NA * NE * NP + NB * NA * NP * NR)
 
-V_COLS = 192
+V_COLS = 224
 
 
 def tile_attributegnn_pa_kernel(
@@ -55,7 +55,6 @@ def tile_attributegnn_pa_kernel(
         a_s = keep.tile([PT, NA * 256], U8, name="a_s", align_bytes=64)
         f_c = keep.tile([PT, NA * 512], U32, name="f_c", align_bytes=64)
         f_s = keep.tile([PT, NA * 512], U8, name="f_s", align_bytes=64)
-        nodeb = keep.tile([PT, 1024], F32, name="nodeb")
 
         for t in range(4):
             nc.sync.dma_start(out=w_sb[:, t * 1024:(t + 1) * 1024], in_=w_v[:, t, :])
@@ -143,36 +142,39 @@ def tile_attributegnn_pa_kernel(
             quantise(e_c[:, a * 256:(a + 1) * 256], e_s[:, a * 256:(a + 1) * 256],
                      live["eg", a][:])
 
-        def stage1(key, h, rc, rs):
+        def s1(a):
             for bt in range(2):
                 acc = psum.tile([PT, 512], F32, name="s1", tag="bank")
                 for t in range(4):
-                    o = t * 256 + h * PT
-                    mx(acc[:, t * PT:(t + 1) * PT], w_c[:, o:o + PT], w_s[:, o:o + PT],
-                       rc[:, bt * PT:(bt + 1) * PT], rs[:, bt * PT:(bt + 1) * PT])
-                live[key, bt] = acc
+                    o = t * 256
+                    nc.tensor.matmul_mx(
+                        out=acc[:, t * PT:(t + 1) * PT],
+                        lhsT=w_c[:, o:o + PT].bitcast(FP8X4), lhsT_scale=w_s[:, o:o + PT],
+                        rhs=img_c[:, bt * PT:(bt + 1) * PT].bitcast(FP8X4),
+                        rhs_scale=img_s[:, bt * PT:(bt + 1) * PT], start=True, stop=False,
+                    )
+                    e0 = a * 256 + bt * PT
+                    nc.tensor.matmul_mx(
+                        out=acc[:, t * PT:(t + 1) * PT],
+                        lhsT=w_c[:, o + PT:o + 2 * PT].bitcast(FP8X4), lhsT_scale=w_s[:, o + PT:o + 2 * PT],
+                        rhs=e_c[:, e0:e0 + PT].bitcast(FP8X4), rhs_scale=e_s[:, e0:e0 + PT],
+                        start=False, stop=True,
+                    )
+                live[("s1", a), bt] = acc
 
-        def n_ev(bt):
+        def a_v1(a, bt):
+            if ("ag", a) not in live:
+                live["ag", a] = rot.tile([PT, 1024], BF16, name="ag", tag="ag", align_bytes=64)
             nc.vector.tensor_tensor(
-                out=nodeb[:, bt * 512:(bt + 1) * 512].rearrange("p (c t) -> p c t", t=4),
-                in0=live["n", bt][:].rearrange("p (t c) -> p c t", t=4),
+                out=live["ag", a][:, bt * 512:(bt + 1) * 512].rearrange("p (c t) -> p c t", t=4),
+                in0=live[("s1", a), bt][:].rearrange("p (t c) -> p c t", t=4),
                 in1=bias_f[:].unsqueeze(1).to_broadcast([PT, PT, 4]),
                 op=ADD,
             )
 
-        def s1(a):
-            stage1(("s1", a), 1, e_c[:, a * 256:(a + 1) * 256], e_s[:, a * 256:(a + 1) * 256])
-
         def a_v(a):
-            ag = rot.tile([PT, 1024], BF16, name="ag", tag="ag", align_bytes=64)
-            for bt in range(2):
-                nc.vector.tensor_tensor(
-                    out=ag[:, bt * 512:(bt + 1) * 512].rearrange("p (c t) -> p c t", t=4),
-                    in0=live[("s1", a), bt][:].rearrange("p (t c) -> p c t", t=4),
-                    in1=nodeb[:, bt * 512:(bt + 1) * 512].rearrange("p (c t) -> p c t", t=4),
-                    op=ADD,
-                )
-            live["ag", a] = ag
+            a_v1(a, 0)
+            a_v1(a, 1)
 
         def q_a(a):
             quantise(a_c[:, a * 256:(a + 1) * 256], a_s[:, a * 256:(a + 1) * 256],
@@ -243,7 +245,6 @@ def tile_attributegnn_pa_kernel(
         t_e(0)
         e_e(0)
         quantise(img_c[:], img_s[:], img_g[:])
-        stage1("n", 0, img_c, img_s)
         t_e(1)
         rg_s(0)
         rg_v(0)
@@ -251,37 +252,40 @@ def tile_attributegnn_pa_kernel(
         s1(0)
         e_e(1)
         rg_v(1)
-        n_ev(0)
-        n_ev(1)
         rg_s(1)
         q_f(0)
+        q_e(1)
 
+        last = NA - 1
         for i in range(NA):
             if i + 2 < NA:
                 t_e(i + 2)
-            a_v(i)
+            if i + 1 < NA:
+                s1(i + 1)
+            if i < last:
+                a_v(i)
             if i >= 2:
                 o_ev(i - 2, "SS", False)
-            if i + 1 < NA:
-                q_e(i + 1)
-                s1(i + 1)
             if i + 2 < NA:
                 rg_s(i + 2)
                 rg_v(i + 2)
-            if i + 1 < NA:
+            if i < last:
                 q_a(i)
                 s2(i)
+            else:
+                a_v1(last, 0)
+                q_a_half(last, 0)
+                acc_a = s2_cols(last, 0, 0, NR)
+                a_v1(last, 1)
+                q_a_half(last, 1)
+                acc_b = s2_cols(last, 1, 0, 256)
+                acc_c = s2_cols(last, 1, 256, NR)
             if i + 2 < NA:
                 e_e(i + 2)
             if i + 1 < NA:
                 q_f(i + 1)
-
-        last = NA - 1
-        q_a_half(last, 0)
-        acc_a = s2_cols(last, 0, 0, NR)
-        q_a_half(last, 1)
-        acc_b = s2_cols(last, 1, 0, 256)
-        acc_c = s2_cols(last, 1, 256, NR)
+            if i + 2 < NA:
+                q_e(i + 2)
 
         o_6 = outp.tile([PT, 1024], F32, name="o_sb", tag="o_sb")
         o_7 = outp.tile([PT, 1024], F32, name="o_sb", tag="o_sb")

from contextlib import ExitStack

import concourse.mybir as mybir
from concourse.masks import make_identity

F32 = mybir.dt.float32
BF16 = mybir.dt.bfloat16
U32 = mybir.dt.uint32
U8 = mybir.dt.uint8
FP8X4 = mybir.dt.float8_e4m3fn_x4
ADD = mybir.AluOpType.add

NB, NA, NE, NP, NR = 256, 8, 512, 512, 512
PT = 128
FLOPS = 2 * (NB * NE * NP + NB * NA * NE * NP + NB * NA * NP * NR)

V_COLS = 224


def tile_attributegnn_pa_kernel(
    tc, image_features, edge_attributes, linear_w, linear_b, fwd_proj, out
):
    nc = tc.nc
    with ExitStack() as ctx:
        keep = ctx.enter_context(tc.tile_pool(name="keep", bufs=1))
        rot = ctx.enter_context(tc.tile_pool(name="rot", bufs=4))
        outp = ctx.enter_context(tc.tile_pool(name="outp", bufs=4))
        psum = ctx.enter_context(tc.psum_pool(name="psum", bufs=8))
        ctx.enter_context(tc.manual_schedule())

        w_v = linear_w.rearrange("(p t) e -> p t e", t=4)
        img_v = image_features.rearrange("(p bt) e -> p (bt e)", bt=2)
        edge_v = edge_attributes.rearrange("(p bt) a e -> p bt (a e)", bt=2)
        fwd_v = fwd_proj.rearrange("a (p t) r -> a p (t r)", t=4)
        b_v = linear_b.rearrange("(p t) -> p t", t=4)
        out_v = out.rearrange("(p bt) a r -> p bt a r", bt=2)

        w_sb = keep.tile([PT, 4 * 1024], BF16, name="w_sb")
        img_sb = keep.tile([PT, 1024], BF16, name="img_sb")
        bias_bf = keep.tile([PT, 4], BF16, name="bias_bf")
        bias_f = keep.tile([PT, 4], F32, name="bias_f")
        e_sb = [keep.tile([PT, 2048], BF16, name="e_sb%d" % q) for q in range(4)]
        f_sb = [keep.tile([PT, 2048], BF16, name="f_sb%d" % a) for a in range(NA)]
        ident = keep.tile([PT, PT], F32, name="ident")

        w_g = keep.tile([PT, 4096], BF16, name="w_g", align_bytes=64)
        w_c = keep.tile([PT, 1024], U32, name="w_c", align_bytes=64)
        w_s = keep.tile([PT, 1024], U8, name="w_s", align_bytes=64)
        img_g = keep.tile([PT, 1024], BF16, name="img_g", align_bytes=64)
        img_c = keep.tile([PT, 256], U32, name="img_c", align_bytes=64)
        img_s = keep.tile([PT, 256], U8, name="img_s", align_bytes=64)
        e_c = keep.tile([PT, NA * 256], U32, name="e_c", align_bytes=64)
        e_s = keep.tile([PT, NA * 256], U8, name="e_s", align_bytes=64)
        a_c = keep.tile([PT, NA * 256], U32, name="a_c", align_bytes=64)
        a_s = keep.tile([PT, NA * 256], U8, name="a_s", align_bytes=64)
        f_c = keep.tile([PT, NA * 512], U32, name="f_c", align_bytes=64)
        f_s = keep.tile([PT, NA * 512], U8, name="f_s", align_bytes=64)

        for t in range(4):
            nc.sync.dma_start(out=w_sb[:, t * 1024:(t + 1) * 1024], in_=w_v[:, t, :])
        nc.sync.dma_start(out=img_sb[:], in_=img_v)
        nc.sync.dma_start(out=bias_bf[:], in_=b_v)

        def load_edge(q):
            nc.sync.dma_start(
                out=e_sb[q][:].rearrange("p (bt x) -> p bt x", bt=2),
                in_=edge_v[:, :, q * 1024:(q + 1) * 1024],
            )

        def load_fwd(a):
            nc.sync.dma_start(out=f_sb[a][:], in_=fwd_v[a])

        for q in range(4):
            load_edge(q)
            load_fwd(2 * q)
            load_fwd(2 * q + 1)

        make_identity(nc, ident[:])

        def transpose_words(dst, src32, cols):
            nc.tensor.transpose(dst, src32[:, cols:cols + PT], ident[:])

        def quantise(codes, scales, grouped):
            nc.vector.quantize_mx(out=codes.bitcast(FP8X4), scales=scales, in_=grouped)

        def mx(acc, lc, ls, rc, rs):
            nc.tensor.matmul_mx(
                out=acc, lhsT=lc.bitcast(FP8X4), lhsT_scale=ls,
                rhs=rc.bitcast(FP8X4), rhs_scale=rs, start=True, stop=True,
            )

        w32 = w_sb[:].bitcast(F32)
        wg32 = w_g[:].bitcast(F32)
        live = {}

        def t_w(t):
            tr = psum.tile([PT, 512], F32, name="tr", tag="bank")
            for hu in range(4):
                transpose_words(tr[:, hu * PT:(hu + 1) * PT], w32, t * 512 + hu * PT)
            live["tw", t] = tr

        def copy_on(eng, out, in_):
            if eng == "V":
                nc.vector.tensor_copy(out=out, in_=in_)
            else:
                nc.scalar.copy(out=out, in_=in_)

        def e_w(t, eng):
            copy_on(
                eng,
                out=wg32[:, t * 512:(t + 1) * 512].rearrange("p (h m u) -> p h m u", h=2, u=2),
                in_=live["tw", t][:].rearrange("p (h u m) -> p h m u", h=2, u=2),
            )

        def q_w(t):
            quantise(w_c[:, t * 256:(t + 1) * 256], w_s[:, t * 256:(t + 1) * 256],
                     w_g[:, t * 1024:(t + 1) * 1024])

        def t_rows(key, src32, stride_bt, base):
            tr = psum.tile([PT, 512], F32, name="tr", tag="bank")
            for u in range(2):
                for bt in range(2):
                    transpose_words(tr[:, u * 256 + bt * PT: u * 256 + (bt + 1) * PT],
                                    src32, bt * stride_bt + base + u * PT)
            live[key] = tr

        def e_rows(key, grouped):
            nc.scalar.copy(
                out=grouped[:].bitcast(F32).rearrange("p (c u) -> p c u", u=2),
                in_=live[key][:].rearrange("p (u c) -> p c u", u=2),
            )

        def t_e(a):
            t_rows(("te", a), e_sb[a // 2][:].bitcast(F32), 512, (a % 2) * 256)

        def e_e(a):
            eg = rot.tile([PT, 1024], BF16, name="eg", tag="eg", align_bytes=64)
            e_rows(("te", a), eg)
            live["eg", a] = eg

        def q_e(a):
            quantise(e_c[:, a * 256:(a + 1) * 256], e_s[:, a * 256:(a + 1) * 256],
                     live["eg", a][:])

        def s1(a):
            for bt in range(2):
                acc = psum.tile([PT, 512], F32, name="s1", tag="bank")
                for t in range(4):
                    o = t * 256
                    nc.tensor.matmul_mx(
                        out=acc[:, t * PT:(t + 1) * PT],
                        lhsT=w_c[:, o:o + PT].bitcast(FP8X4), lhsT_scale=w_s[:, o:o + PT],
                        rhs=img_c[:, bt * PT:(bt + 1) * PT].bitcast(FP8X4),
                        rhs_scale=img_s[:, bt * PT:(bt + 1) * PT], start=True, stop=False,
                    )
                    e0 = a * 256 + bt * PT
                    nc.tensor.matmul_mx(
                        out=acc[:, t * PT:(t + 1) * PT],
                        lhsT=w_c[:, o + PT:o + 2 * PT].bitcast(FP8X4), lhsT_scale=w_s[:, o + PT:o + 2 * PT],
                        rhs=e_c[:, e0:e0 + PT].bitcast(FP8X4), rhs_scale=e_s[:, e0:e0 + PT],
                        start=False, stop=True,
                    )
                live[("s1", a), bt] = acc

        def a_v1(a, bt):
            if ("ag", a) not in live:
                live["ag", a] = rot.tile([PT, 1024], BF16, name="ag", tag="ag", align_bytes=64)
            nc.vector.tensor_tensor(
                out=live["ag", a][:, bt * 512:(bt + 1) * 512].rearrange("p (c t) -> p c t", t=4),
                in0=live[("s1", a), bt][:].rearrange("p (t c) -> p c t", t=4),
                in1=bias_f[:].unsqueeze(1).to_broadcast([PT, PT, 4]),
                op=ADD,
            )

        def a_v(a):
            a_v1(a, 0)
            a_v1(a, 1)

        def q_a(a):
            quantise(a_c[:, a * 256:(a + 1) * 256], a_s[:, a * 256:(a + 1) * 256],
                     live["ag", a][:])

        def q_a_half(a, bt):
            o = a * 256 + bt * PT
            quantise(a_c[:, o:o + PT], a_s[:, o:o + PT], live["ag", a][:, bt * 512:(bt + 1) * 512])

        def rg_views(a, r0, r1):
            if ("fg", a) not in live:
                live["fg", a] = rot.tile([PT, 2048], BF16, name="fg", tag="fg", align_bytes=64)
            fg = live["fg", a]
            dst = fg[:, r0 * 4:r1 * 4].rearrange("p (c i t) -> p c t i", i=4, t=4)
            src = f_sb[a][:].rearrange("p (t r) -> p t r", t=4)[:, :, r0:r1].rearrange(
                "p t (c i) -> p c t i", i=4)
            return dst, src

        def rg_s(a):
            dst, src = rg_views(a, V_COLS, NR)
            nc.scalar.copy(out=dst, in_=src)

        def rg_v(a):
            dst, src = rg_views(a, 0, V_COLS)
            nc.vector.tensor_copy(out=dst, in_=src)

        def q_f(a):
            quantise(f_c[:, a * 512:(a + 1) * 512], f_s[:, a * 512:(a + 1) * 512],
                     live["fg", a][:])

        def s2_cols(a, bt, c0, c1):
            acc = psum.tile([PT, 512], F32, name="s2", tag="bank")
            o = a * 256 + bt * PT
            mx(acc[:, 0:c1 - c0], a_c[:, o:o + PT], a_s[:, o:o + PT],
               f_c[:, a * 512 + c0:a * 512 + c1], f_s[:, a * 512 + c0:a * 512 + c1])
            return acc

        def s2(a):
            for bt in range(2):
                live["s2", a, bt] = s2_cols(a, bt, 0, NR)

        def o_ev(a, engines, split_store):
            o_sb = outp.tile([PT, 1024], F32, name="o_sb", tag="o_sb")
            for bt in range(2):
                copy_on(engines[bt], out=o_sb[:, bt * 512:(bt + 1) * 512], in_=live["s2", a, bt][:])
            if split_store:
                for bt in range(2):
                    nc.sync.dma_start(out=out_v[:, bt, a, :], in_=o_sb[:, bt * 512:(bt + 1) * 512])
            else:
                nc.sync.dma_start(out=out_v[:, :, a, :],
                                  in_=o_sb[:].rearrange("p (bt r) -> p bt r", bt=2))

        t_w(0)
        e_w(0, "S")
        t_w(1)
        e_w(1, "V")
        q_w(0)
        t_w(2)
        e_w(2, "S")
        q_w(1)
        t_w(3)
        e_w(3, "V")
        q_w(2)
        t_rows("ti", img_sb[:].bitcast(F32), 256, 0)
        e_rows("ti", img_g)
        q_w(3)
        nc.vector.tensor_copy(out=bias_f[:], in_=bias_bf[:])
        t_e(0)
        e_e(0)
        quantise(img_c[:], img_s[:], img_g[:])
        t_e(1)
        rg_s(0)
        rg_v(0)
        q_e(0)
        s1(0)
        e_e(1)
        rg_v(1)
        rg_s(1)
        q_f(0)
        q_e(1)

        last = NA - 1
        for i in range(NA):
            if i + 2 < NA:
                t_e(i + 2)
            if i + 1 < NA:
                s1(i + 1)
            if i < last:
                a_v(i)
            if i >= 2:
                o_ev(i - 2, "SS", False)
            if i + 2 < NA:
                rg_s(i + 2)
                rg_v(i + 2)
            if i < last:
                q_a(i)
                s2(i)
            else:
                a_v1(last, 0)
                q_a_half(last, 0)
                acc_a = s2_cols(last, 0, 0, NR)
                a_v1(last, 1)
                q_a_half(last, 1)
                acc_b = s2_cols(last, 1, 0, 256)
                acc_c = s2_cols(last, 1, 256, NR)
            if i + 2 < NA:
                e_e(i + 2)
            if i + 1 < NA:
                q_f(i + 1)
            if i + 2 < NA:
                q_e(i + 2)

        o_6 = outp.tile([PT, 1024], F32, name="o_sb", tag="o_sb")
        o_7 = outp.tile([PT, 1024], F32, name="o_sb", tag="o_sb")
        nc.scalar.copy(out=o_6[:, 0:512], in_=live["s2", last - 1, 0][:])
        nc.sync.dma_start(out=out_v[:, 0, last - 1, :], in_=o_6[:, 0:512])
        nc.vector.tensor_copy(out=o_6[:, 512:1024], in_=live["s2", last - 1, 1][:])
        nc.sync.dma_start(out=out_v[:, 1, last - 1, :], in_=o_6[:, 512:1024])
        nc.scalar.copy(out=o_7[:, 0:512], in_=acc_a[:])
        nc.sync.dma_start(out=out_v[:, 0, last, :], in_=o_7[:, 0:512])
        nc.vector.tensor_copy(out=o_7[:, 512:768], in_=acc_b[:, 0:256])
        nc.sync.dma_start(out=out_v[:, 1, last, 0:256], in_=o_7[:, 512:768])
        nc.scalar.copy(out=o_7[:, 768:1024], in_=acc_c[:, 0:256])
        nc.sync.dma_start(out=out_v[:, 1, last, 256:512], in_=o_7[:, 768:1024])
